import numpy as np
import ml_dtypes


def mxq(x, axis, fmt="e4m3"):
    dtype, down = {"e4m3": (ml_dtypes.float8_e4m3fn, 7), "e5m2": (ml_dtypes.float8_e5m2, 14)}[fmt]
    v = np.moveaxis(np.asarray(x, np.float32).astype(ml_dtypes.bfloat16).astype(np.float64), axis, -1)
    blocks = v.reshape(v.shape[:-1] + (-1, 32))
    amax = np.abs(blocks).max(-1, keepdims=True)
    byte = np.maximum(np.where(amax > 0, np.frexp(amax)[1] - 1 + 127, 0) - down, 1)
    scale = np.exp2(byte - 127.0)
    codes = (blocks / scale).astype(np.float32).astype(dtype).astype(np.float64)
    return np.moveaxis((codes * scale).reshape(v.shape), -1, axis)


WIDE = False


def mx_kscale(k):
    if not WIDE:
        return np.ones(k)
    levels = np.array([20, -20, 10, -10, 0])
    a = np.random.permutation(np.resize(levels, k // 512 * 4)).reshape(k // 512, 4)
    idx = np.arange(k)
    return np.exp2(a[idx // 512, idx % 128 // 32])


BF16 = ml_dtypes.bfloat16


def bf(x):
    return np.asarray(x, np.float32).astype(BF16)


def f64(x):
    return np.asarray(x).astype(np.float64)


B, T, D, E, H, L = 64, 10, 512, 128, 128, 2
TM = T - L
F = H + L * D + 1


def setup_inputs():
    u = mx_kscale(D)
    we = np.random.standard_normal((D, H)) / np.sqrt(H) / u[:, None]
    wy = np.random.standard_normal((D, L, D)) * 0.7 / np.sqrt(L * D) / u[:, None, None]
    wx = np.random.standard_normal((D, 1)) * 0.5 / u[:, None]
    x = np.random.standard_normal((B, T, D))
    emb = np.random.standard_normal((B, H)) * 0.5
    bg = np.random.standard_normal(D) * 0.3 / u
    g = np.random.standard_normal((B, TM, D)) * np.exp2(np.random.randint(-12, 1, (B, TM, 1))) * 4.0 * u
    return {"x": bf(x),
            "emb": bf(emb),
            "Wg": bf(np.concatenate([we, wy.reshape(D, L * D), wx], axis=1)),
            "bg": bf(bg),
            "grad_out": bf(g)}


def reference(x, emb, Wg, bg, grad_out):
    g = f64(grad_out)
    Wy = f64(Wg)[:, H:H + L * D].reshape(D, L, D)
    wx = f64(Wg)[:, -1]
    gq = mxq(g, 2, "e5m2")
    wq = mxq(Wy, 0, "e4m3")
    gx = np.zeros((B, T, D))
    for l in range(L):
        gx[:, l:TM + l, :] += (gq @ wq[:, l, :])
    gx[:, L:, :] += g * wx
    return gx

@@ -1,0 +1,153 @@
+from contextlib import ExitStack
+
+import concourse.mybir as mybir
+from concourse.masks import make_identity
+
+F32 = mybir.dt.float32
+BF16 = mybir.dt.bfloat16
+U32 = mybir.dt.uint32
+U8 = mybir.dt.uint8
+I32 = mybir.dt.int32
+E4M3_X4 = mybir.dt.float8_e4m3fn_x4
+E5M2_X4 = mybir.dt.float8_e5m2_x4
+MULT = mybir.AluOpType.mult
+ADD = mybir.AluOpType.add
+
+P = 128
+PACK = 4
+BATCH = 64
+STEPS_IN = 8
+STEPS_OUT = 10
+LATENT = 512
+LAGS = 2
+WY_COLUMN = 128
+WX_COLUMN = WY_COLUMN + LAGS * LATENT
+STEPS_PER_TILE = P // BATCH
+IN_TILES = STEPS_IN // STEPS_PER_TILE
+OUT_TILES = STEPS_OUT // STEPS_PER_TILE
+WORDS = LATENT // 2
+
+FLOPS = 2 * BATCH * STEPS_IN * LATENT * LAGS * LATENT
+BYTES = 2 * LATENT * (LAGS * LATENT + 1) + 2 * BATCH * STEPS_IN * LATENT + 4 * BATCH * STEPS_OUT * LATENT
+
+
+def tile_npchangetransitionprior_pa_s_kernel(tc, x, emb, Wg, bg, grad_out, out):
+    nc = tc.nc
+    with ExitStack() as ctx:
+        keep = ctx.enter_context(tc.tile_pool(name="keep", bufs=1))
+        psum = ctx.enter_context(tc.psum_pool(name="psum", bufs=1))
+
+        wx_sb = keep.tile([P, PACK], BF16)
+        with nc.allow_non_contiguous_dma(reason="wx is one column of Wg: 512 single elements"):
+            nc.scalar.dma_start(
+                out=wx_sb[:],
+                in_=Wg[:, WX_COLUMN : WX_COLUMN + 1].rearrange("(c q) o -> q (c o)", q=P),
+            )
+
+        g_sb = keep.tile([P, IN_TILES, LATENT], BF16)
+        g_by_parity = grad_out.rearrange("b (m e) d -> e b m d", e=STEPS_PER_TILE)
+        for first in range(0, IN_TILES, 2):
+            for e in range(STEPS_PER_TILE):
+                nc.sync.dma_start(
+                    out=g_sb[e * BATCH : (e + 1) * BATCH, first : first + 2, :],
+                    in_=g_by_parity[e][:, first : first + 2, :],
+                )
+
+        w_raw = []
+        for lag in range(LAGS):
+            raw = keep.tile([P, PACK, LATENT], BF16, name="w_raw%d" % lag)
+            first_column = WY_COLUMN + lag * LATENT
+            nc.sync.dma_start(
+                out=raw[:],
+                in_=Wg[:, first_column : first_column + LATENT].rearrange("(p t) j -> p t j", t=PACK),
+            )
+            w_raw.append(raw)
+
+        ident_f32 = keep.tile([P, P], F32)
+        make_identity(nc, ident_f32[:])
+        ident_bf16 = keep.tile([P, P], BF16)
+        make_identity(nc, ident_bf16[:])
+
+        g_columns = (STEPS_IN + 2) * BATCH
+        g_codes = keep.tile([P, g_columns], U32, align_bytes=64)
+        g_scales = keep.tile([P, g_columns], U8, align_bytes=64)
+        nc.vector.memset(g_codes[:].bitcast(I32), 0)
+        nc.vector.memset(g_scales[:].bitcast(I32), 0)
+
+        wx_all = psum.tile([P, LATENT], F32)
+        for c in range(PACK):
+            nc.tensor.matmul(
+                out=wx_all[:, c * P : (c + 1) * P],
+                lhsT=wx_sb[:, c : c + 1].to_broadcast([P, P]),
+                rhs=ident_bf16[:],
+                start=True,
+                stop=True,
+            )
+
+        g_words = g_sb[:].bitcast(F32).rearrange("r m (q u) -> r m u q", u=2)
+        g_grouped = keep.tile([P, STEPS_IN * BATCH, PACK], BF16, align_bytes=64)
+        g_grouped_words = g_grouped[:].bitcast(F32).rearrange("q (m r) u -> q m r u", r=P)
+        for first in range(0, IN_TILES, 2):
+            flipped = psum.tile([P, 2, 2, P], F32, name="flipped%d" % first)
+            for i in range(2):
+                for u in range(2):
+                    nc.tensor.transpose(flipped[:, i, u, :], g_words[:, first + i, u, :], ident_f32[:])
+            nc.scalar.copy(
+                out=g_grouped_words[:, first : first + 2, :, :],
+                in_=flipped[:].rearrange("q m u r -> q m r u"),
+            )
+
+        third = [None]
+        for m in range(1, OUT_TILES):
+            product = keep.tile([P, LATENT], F32, name="third%d" % m)
+            nc.vector.tensor_tensor(out=product[:], in0=g_sb[:, m - 1, :], in1=wx_all[:], op=MULT)
+            third.append(product)
+
+        for first in range(0, IN_TILES, 2):
+            tokens = slice(first * P, (first + 2) * P)
+            columns = slice(BATCH + first * P, BATCH + (first + 2) * P)
+            nc.vector.quantize_mx(
+                out=g_codes[:, columns].bitcast(E5M2_X4),
+                scales=g_scales[:, columns],
+                in_=g_grouped[:, tokens, :].rearrange("q r t -> q (r t)"),
+            )
+
+        w_codes = keep.tile([P, LAGS, LATENT], U32, align_bytes=64)
+        w_scales = keep.tile([P, LAGS, LATENT], U8, align_bytes=64)
+        w_grouped = []
+        for lag in range(LAGS):
+            grouped = keep.tile([P, LATENT, PACK], BF16, name="w_grouped%d" % lag, align_bytes=64)
+            nc.vector.tensor_copy(
+                out=grouped[:].rearrange("p (c i) t -> p c t i", i=4),
+                in_=w_raw[lag][:].rearrange("p t (c i) -> p c t i", i=4),
+            )
+            w_grouped.append(grouped)
+        for lag in range(LAGS):
+            nc.vector.quantize_mx(
+                out=w_codes[:, lag, :].bitcast(E4M3_X4),
+                scales=w_scales[:, lag, :],
+                in_=w_grouped[lag][:].rearrange("p j t -> p (j t)"),
+            )
+
+        for m in range(OUT_TILES):
+            lags = [lag for lag in range(LAGS) if m * STEPS_PER_TILE - lag < STEPS_IN]
+            acc = psum.tile([P, LATENT], F32, name="acc%d" % m)
+            for lag in lags:
+                start_column = BATCH + m * P - lag * BATCH
+                window = slice(start_column, start_column + P)
+                nc.tensor.matmul_mx(
+                    out=acc[:],
+                    lhsT=g_codes[:, window].bitcast(E5M2_X4),
+                    lhsT_scale=g_scales[:, window],
+                    rhs=w_codes[:, lag, :].bitcast(E4M3_X4),
+                    rhs_scale=w_scales[:, lag, :],
+                    start=(lag == lags[0]),
+                    stop=(lag == lags[-1]),
+                )
+            result = keep.tile([P, LATENT], F32, name="result%d" % m)
+            if m == 0:
+                nc.scalar.copy(out=result[:], in_=acc[:])
+            else:
+                nc.vector.tensor_tensor(out=result[:], in0=acc[:], in1=third[m][:], op=ADD)
+            nc.sync.dma_start(out=out[:, m * STEPS_PER_TILE, :], in_=result[0:BATCH, :])
+            nc.scalar.dma_start(out=out[:, m * STEPS_PER_TILE + 1, :], in_=result[BATCH:P, :])

@@ -7,7 +7,6 @@ F32 = mybir.dt.float32
 BF16 = mybir.dt.bfloat16
 U32 = mybir.dt.uint32
 U8 = mybir.dt.uint8
-I32 = mybir.dt.int32
 E4M3_X4 = mybir.dt.float8_e4m3fn_x4
 E5M2_X4 = mybir.dt.float8_e5m2_x4
 MULT = mybir.AluOpType.mult
@@ -22,13 +21,15 @@ LATENT = 512
 LAGS = 2
 WY_COLUMN = 128
 WX_COLUMN = WY_COLUMN + LAGS * LATENT
-STEPS_PER_TILE = P // BATCH
-IN_TILES = STEPS_IN // STEPS_PER_TILE
-OUT_TILES = STEPS_OUT // STEPS_PER_TILE
-WORDS = LATENT // 2
+HALVES = P // BATCH
+OUT_TILES = STEPS_OUT // HALVES
+SLOTS = OUT_TILES + LAGS
+MX_SLOTS = SLOTS - 1
 
 FLOPS = 2 * BATCH * STEPS_IN * LATENT * LAGS * LATENT
 BYTES = 2 * LATENT * (LAGS * LATENT + 1) + 2 * BATCH * STEPS_IN * LATENT + 4 * BATCH * STEPS_OUT * LATENT
+
+SCALAR_COLUMNS = 160
 
 
 def tile_npchangetransitionprior_pa_s_kernel(tc, x, emb, Wg, bg, grad_out, out):
@@ -36,6 +37,7 @@ def tile_npchangetransitionprior_pa_s_kernel(tc, x, emb, Wg, bg, grad_out, out):
     with ExitStack() as ctx:
         keep = ctx.enter_context(tc.tile_pool(name="keep", bufs=1))
         psum = ctx.enter_context(tc.psum_pool(name="psum", bufs=1))
+        psum_flip = ctx.enter_context(tc.psum_pool(name="psum_flip", bufs=2))
 
         wx_sb = keep.tile([P, PACK], BF16)
         with nc.allow_non_contiguous_dma(reason="wx is one column of Wg: 512 single elements"):
@@ -44,14 +46,17 @@ def tile_npchangetransitionprior_pa_s_kernel(tc, x, emb, Wg, bg, grad_out, out):
                 in_=Wg[:, WX_COLUMN : WX_COLUMN + 1].rearrange("(c q) o -> q (c o)", q=P),
             )
 
-        g_sb = keep.tile([P, IN_TILES, LATENT], BF16)
-        g_by_parity = grad_out.rearrange("b (m e) d -> e b m d", e=STEPS_PER_TILE)
-        for first in range(0, IN_TILES, 2):
-            for e in range(STEPS_PER_TILE):
-                nc.sync.dma_start(
-                    out=g_sb[e * BATCH : (e + 1) * BATCH, first : first + 2, :],
-                    in_=g_by_parity[e][:, first : first + 2, :],
-                )
+        g_slots = keep.tile([P, SLOTS, LATENT], BF16)
+        nc.vector.memset(g_slots[:, 0:LAGS, :], 0.0)
+        nc.vector.memset(g_slots[:, OUT_TILES:SLOTS, :], 0.0)
+        for h in reversed(range(HALVES)):
+            step_of_slot_0 = h * OUT_TILES - LAGS
+            first_step = max(0, step_of_slot_0)
+            end_step = min(STEPS_IN, step_of_slot_0 + SLOTS)
+            nc.sync.dma_start(
+                out=g_slots[h:P:HALVES, first_step - step_of_slot_0 : end_step - step_of_slot_0, :],
+                in_=grad_out[:, first_step:end_step, :],
+            )
 
         w_raw = []
         for lag in range(LAGS):
@@ -63,16 +68,10 @@ def tile_npchangetransitionprior_pa_s_kernel(tc, x, emb, Wg, bg, grad_out, out):
             )
             w_raw.append(raw)
 
-        ident_f32 = keep.tile([P, P], F32)
-        make_identity(nc, ident_f32[:])
         ident_bf16 = keep.tile([P, P], BF16)
         make_identity(nc, ident_bf16[:])
-
-        g_columns = (STEPS_IN + 2) * BATCH
-        g_codes = keep.tile([P, g_columns], U32, align_bytes=64)
-        g_scales = keep.tile([P, g_columns], U8, align_bytes=64)
-        nc.vector.memset(g_codes[:].bitcast(I32), 0)
-        nc.vector.memset(g_scales[:].bitcast(I32), 0)
+        ident_f32 = keep.tile([P, P], F32)
+        make_identity(nc, ident_f32[:])
 
         wx_all = psum.tile([P, LATENT], F32)
         for c in range(PACK):
@@ -84,70 +83,80 @@ def tile_npchangetransitionprior_pa_s_kernel(tc, x, emb, Wg, bg, grad_out, out):
                 stop=True,
             )
 
-        g_words = g_sb[:].bitcast(F32).rearrange("r m (q u) -> r m u q", u=2)
-        g_grouped = keep.tile([P, STEPS_IN * BATCH, PACK], BF16, align_bytes=64)
-        g_grouped_words = g_grouped[:].bitcast(F32).rearrange("q (m r) u -> q m r u", r=P)
-        for first in range(0, IN_TILES, 2):
-            flipped = psum.tile([P, 2, 2, P], F32, name="flipped%d" % first)
-            for i in range(2):
+        g_words = g_slots[:].bitcast(F32).rearrange("r v (q u) -> r v u q", u=2)
+        g_grouped = keep.tile([P, MX_SLOTS * P, PACK], BF16, align_bytes=64)
+        g_grouped_words = g_grouped[:].bitcast(F32).rearrange("q (v r) u -> q v r u", r=P)
+        for first in range(0, MX_SLOTS, 2):
+            flipped = psum_flip.tile([P, 2, 2, P], F32)
+            for n in range(2):
                 for u in range(2):
-                    nc.tensor.transpose(flipped[:, i, u, :], g_words[:, first + i, u, :], ident_f32[:])
+                    nc.tensor.transpose(flipped[:, n, u, :], g_words[:, 1 + first + n, u, :], ident_f32[:])
             nc.scalar.copy(
                 out=g_grouped_words[:, first : first + 2, :, :],
-                in_=flipped[:].rearrange("q m u r -> q m r u"),
+                in_=flipped[:].rearrange("q v u r -> q v r u"),
             )
 
-        third = [None]
-        for m in range(1, OUT_TILES):
-            product = keep.tile([P, LATENT], F32, name="third%d" % m)
-            nc.vector.tensor_tensor(out=product[:], in0=g_sb[:, m - 1, :], in1=wx_all[:], op=MULT)
-            third.append(product)
+        own = []
 
-        for first in range(0, IN_TILES, 2):
-            tokens = slice(first * P, (first + 2) * P)
-            columns = slice(BATCH + first * P, BATCH + (first + 2) * P)
+        def own_latent_term(i):
+            product = keep.tile([P, LATENT], F32, name="own%d" % i)
+            nc.vector.tensor_tensor(out=product[:], in0=g_slots[:, i, :], in1=wx_all[:], op=MULT)
+            own.append(product)
+
+        for i in range(3):
+            own_latent_term(i)
+
+        w_grouped = []
+        for lag in range(LAGS):
+            grouped = keep.tile([P, LATENT, PACK], BF16, name="w_grouped%d" % lag, align_bytes=64)
+            split = LATENT - SCALAR_COLUMNS
+            nc.vector.tensor_copy(
+                out=grouped[:, 0:split, :].rearrange("p (c n) t -> p c t n", n=4),
+                in_=w_raw[lag][:, :, 0:split].rearrange("p t (c n) -> p c t n", n=4),
+            )
+            nc.scalar.copy(
+                out=grouped[:, split:LATENT, :].rearrange("p (c n) t -> p c t n", n=4),
+                in_=w_raw[lag][:, :, split:LATENT].rearrange("p t (c n) -> p c t n", n=4),
+            )
+            w_grouped.append(grouped)
+
+        g_codes = keep.tile([P, MX_SLOTS * P], U32, align_bytes=64)
+        g_scales = keep.tile([P, MX_SLOTS * P], U8, align_bytes=64)
+        for first in range(0, MX_SLOTS, 2):
+            columns = slice(first * P, (first + 2) * P)
             nc.vector.quantize_mx(
                 out=g_codes[:, columns].bitcast(E5M2_X4),
                 scales=g_scales[:, columns],
-                in_=g_grouped[:, tokens, :].rearrange("q r t -> q (r t)"),
+                in_=g_grouped[:, columns, :].rearrange("q r t -> q (r t)"),
             )
 
         w_codes = keep.tile([P, LAGS, LATENT], U32, align_bytes=64)
         w_scales = keep.tile([P, LAGS, LATENT], U8, align_bytes=64)
-        w_grouped = []
-        for lag in range(LAGS):
-            grouped = keep.tile([P, LATENT, PACK], BF16, name="w_grouped%d" % lag, align_bytes=64)
-            nc.vector.tensor_copy(
-                out=grouped[:].rearrange("p (c i) t -> p c t i", i=4),
-                in_=w_raw[lag][:].rearrange("p t (c i) -> p c t i", i=4),
-            )
-            w_grouped.append(grouped)
+        acc = [psum.tile([P, LATENT], F32, name="acc%d" % i) for i in range(OUT_TILES)]
         for lag in range(LAGS):
             nc.vector.quantize_mx(
                 out=w_codes[:, lag, :].bitcast(E4M3_X4),
                 scales=w_scales[:, lag, :],
                 in_=w_grouped[lag][:].rearrange("p j t -> p (j t)"),
             )
-
-        for m in range(OUT_TILES):
-            lags = [lag for lag in range(LAGS) if m * STEPS_PER_TILE - lag < STEPS_IN]
-            acc = psum.tile([P, LATENT], F32, name="acc%d" % m)
-            for lag in lags:
-                start_column = BATCH + m * P - lag * BATCH
-                window = slice(start_column, start_column + P)
+            for i in range(OUT_TILES):
+                slot = i + LAGS - lag
+                columns = slice((slot - 1) * P, slot * P)
                 nc.tensor.matmul_mx(
-                    out=acc[:],
-                    lhsT=g_codes[:, window].bitcast(E5M2_X4),
-                    lhsT_scale=g_scales[:, window],
+                    out=acc[i][:],
+                    lhsT=g_codes[:, columns].bitcast(E5M2_X4),
+                    lhsT_scale=g_scales[:, columns],
                     rhs=w_codes[:, lag, :].bitcast(E4M3_X4),
                     rhs_scale=w_scales[:, lag, :],
-                    start=(lag == lags[0]),
-                    stop=(lag == lags[-1]),
+                    start=(lag == 0),
+                    stop=(lag == LAGS - 1),
                 )
-            result = keep.tile([P, LATENT], F32, name="result%d" % m)
-            if m == 0:
-                nc.scalar.copy(out=result[:], in_=acc[:])
-            else:
-                nc.vector.tensor_tensor(out=result[:], in0=acc[:], in1=third[m][:], op=ADD)
-            nc.sync.dma_start(out=out[:, m * STEPS_PER_TILE, :], in_=result[0:BATCH, :])
-            nc.scalar.dma_start(out=out[:, m * STEPS_PER_TILE + 1, :], in_=result[BATCH:P, :])
+
+        for i in range(3, OUT_TILES):
+            own_latent_term(i)
+
+        out_rows = out.rearrange("b (h i) j -> (b h) i j", h=HALVES)
+        for i in range(OUT_TILES):
+            result = keep.tile([P, LATENT], F32, name="result%d" % i)
+            nc.vector.tensor_tensor(out=result[:], in0=acc[i][:], in1=own[i][:], op=ADD)
+            nc.sync.dma_start(out=out_rows[:, i, :], in_=result[:])

@@ -30,6 +30,7 @@ FLOPS = 2 * BATCH * STEPS_IN * LATENT * LAGS * LATENT
 BYTES = 2 * LATENT * (LAGS * LATENT + 1) + 2 * BATCH * STEPS_IN * LATENT + 4 * BATCH * STEPS_OUT * LATENT
 
 SCALAR_COLUMNS = 160
+SIDE_TILE = 0
 
 
 def tile_npchangetransitionprior_pa_s_kernel(tc, x, emb, Wg, bg, grad_out, out):
@@ -38,107 +39,85 @@ def tile_npchangetransitionprior_pa_s_kernel(tc, x, emb, Wg, bg, grad_out, out):
         keep = ctx.enter_context(tc.tile_pool(name="keep", bufs=1))
         psum = ctx.enter_context(tc.psum_pool(name="psum", bufs=1))
         psum_flip = ctx.enter_context(tc.psum_pool(name="psum_flip", bufs=2))
+        ctx.enter_context(tc.manual_schedule())
 
         wx_sb = keep.tile([P, PACK], BF16)
-        with nc.allow_non_contiguous_dma(reason="wx is one column of Wg: 512 single elements"):
-            nc.scalar.dma_start(
-                out=wx_sb[:],
-                in_=Wg[:, WX_COLUMN : WX_COLUMN + 1].rearrange("(c q) o -> q (c o)", q=P),
-            )
-
         g_slots = keep.tile([P, SLOTS, LATENT], BF16)
-        nc.vector.memset(g_slots[:, 0:LAGS, :], 0.0)
-        nc.vector.memset(g_slots[:, OUT_TILES:SLOTS, :], 0.0)
-        for h in reversed(range(HALVES)):
-            step_of_slot_0 = h * OUT_TILES - LAGS
-            first_step = max(0, step_of_slot_0)
-            end_step = min(STEPS_IN, step_of_slot_0 + SLOTS)
-            nc.sync.dma_start(
-                out=g_slots[h:P:HALVES, first_step - step_of_slot_0 : end_step - step_of_slot_0, :],
-                in_=grad_out[:, first_step:end_step, :],
-            )
-
-        w_raw = []
-        for lag in range(LAGS):
-            raw = keep.tile([P, PACK, LATENT], BF16, name="w_raw%d" % lag)
-            first_column = WY_COLUMN + lag * LATENT
-            nc.sync.dma_start(
-                out=raw[:],
-                in_=Wg[:, first_column : first_column + LATENT].rearrange("(p t) j -> p t j", t=PACK),
-            )
-            w_raw.append(raw)
-
+        w_raw = [keep.tile([P, PACK, LATENT], BF16, name="w_raw%d" % lag) for lag in range(LAGS)]
         ident_bf16 = keep.tile([P, P], BF16)
-        make_identity(nc, ident_bf16[:])
         ident_f32 = keep.tile([P, P], F32)
-        make_identity(nc, ident_f32[:])
-
         wx_all = psum.tile([P, LATENT], F32)
-        for c in range(PACK):
-            nc.tensor.matmul(
-                out=wx_all[:, c * P : (c + 1) * P],
-                lhsT=wx_sb[:, c : c + 1].to_broadcast([P, P]),
-                rhs=ident_bf16[:],
-                start=True,
-                stop=True,
-            )
+        g_grouped = keep.tile([P, MX_SLOTS * P, PACK], BF16, align_bytes=64)
+        g_codes = keep.tile([P, MX_SLOTS * P], U32, align_bytes=64)
+        g_scales = keep.tile([P, MX_SLOTS * P], U8, align_bytes=64)
+        w_grouped = [
+            keep.tile([P, LATENT, PACK], BF16, name="w_grouped%d" % lag, align_bytes=64) for lag in range(LAGS)
+        ]
+        w_codes = keep.tile([P, LAGS, LATENT], U32, align_bytes=64)
+        w_scales = keep.tile([P, LAGS, LATENT], U8, align_bytes=64)
+        acc = [psum.tile([P, LATENT], F32, name="acc%d" % i) for i in range(OUT_TILES)]
+        own = [keep.tile([P, LATENT], F32, name="own%d" % i) for i in range(OUT_TILES)]
+        result = [keep.tile([P, LATENT], F32, name="result%d" % i) for i in range(OUT_TILES)]
+        side_sum = keep.tile([P, LATENT], F32)
 
         g_words = g_slots[:].bitcast(F32).rearrange("r v (q u) -> r v u q", u=2)
-        g_grouped = keep.tile([P, MX_SLOTS * P, PACK], BF16, align_bytes=64)
         g_grouped_words = g_grouped[:].bitcast(F32).rearrange("q (v r) u -> q v r u", r=P)
-        for first in range(0, MX_SLOTS, 2):
+        out_rows = out.rearrange("b (h i) j -> (b h) i j", h=HALVES)
+
+        def load_slots(first_slot, end_slot):
+            for h in range(HALVES):
+                first_step = h * OUT_TILES - LAGS + first_slot
+                end_step = h * OUT_TILES - LAGS + end_slot
+                if 0 <= first_step and end_step <= STEPS_IN:
+                    nc.sync.dma_start(
+                        out=g_slots[h:P:HALVES, first_slot:end_slot, :],
+                        in_=grad_out[:, first_step:end_step, :],
+                    )
+
+        def load_wy(lag):
+            first_column = WY_COLUMN + lag * LATENT
+            nc.sync.dma_start(
+                out=w_raw[lag][:],
+                in_=Wg[:, first_column : first_column + LATENT].rearrange("(p t) j -> p t j", t=PACK),
+            )
+
+        def flip_slots(pair):
             flipped = psum_flip.tile([P, 2, 2, P], F32)
             for n in range(2):
                 for u in range(2):
-                    nc.tensor.transpose(flipped[:, n, u, :], g_words[:, 1 + first + n, u, :], ident_f32[:])
+                    nc.tensor.transpose(flipped[:, n, u, :], g_words[:, 1 + 2 * pair + n, u, :], ident_f32[:])
             nc.scalar.copy(
-                out=g_grouped_words[:, first : first + 2, :, :],
+                out=g_grouped_words[:, 2 * pair : 2 * pair + 2, :, :],
                 in_=flipped[:].rearrange("q v u r -> q v r u"),
             )
 
-        own = []
-
-        def own_latent_term(i):
-            product = keep.tile([P, LATENT], F32, name="own%d" % i)
-            nc.vector.tensor_tensor(out=product[:], in0=g_slots[:, i, :], in1=wx_all[:], op=MULT)
-            own.append(product)
-
-        for i in range(3):
-            own_latent_term(i)
-
-        w_grouped = []
-        for lag in range(LAGS):
-            grouped = keep.tile([P, LATENT, PACK], BF16, name="w_grouped%d" % lag, align_bytes=64)
-            split = LATENT - SCALAR_COLUMNS
-            nc.vector.tensor_copy(
-                out=grouped[:, 0:split, :].rearrange("p (c n) t -> p c t n", n=4),
-                in_=w_raw[lag][:, :, 0:split].rearrange("p t (c n) -> p c t n", n=4),
-            )
-            nc.scalar.copy(
-                out=grouped[:, split:LATENT, :].rearrange("p (c n) t -> p c t n", n=4),
-                in_=w_raw[lag][:, :, split:LATENT].rearrange("p t (c n) -> p c t n", n=4),
-            )
-            w_grouped.append(grouped)
-
-        g_codes = keep.tile([P, MX_SLOTS * P], U32, align_bytes=64)
-        g_scales = keep.tile([P, MX_SLOTS * P], U8, align_bytes=64)
-        for first in range(0, MX_SLOTS, 2):
-            columns = slice(first * P, (first + 2) * P)
+        def quantise_slots(pair):
+            columns = slice(2 * pair * P, (2 * pair + 2) * P)
             nc.vector.quantize_mx(
                 out=g_codes[:, columns].bitcast(E5M2_X4),
                 scales=g_scales[:, columns],
                 in_=g_grouped[:, columns, :].rearrange("q r t -> q (r t)"),
             )
 
-        w_codes = keep.tile([P, LAGS, LATENT], U32, align_bytes=64)
-        w_scales = keep.tile([P, LAGS, LATENT], U8, align_bytes=64)
-        acc = [psum.tile([P, LATENT], F32, name="acc%d" % i) for i in range(OUT_TILES)]
-        for lag in range(LAGS):
+        def regroup_wy(lag):
+            split = LATENT - SCALAR_COLUMNS
+            nc.vector.tensor_copy(
+                out=w_grouped[lag][:, 0:split, :].rearrange("p (c n) t -> p c t n", n=4),
+                in_=w_raw[lag][:, :, 0:split].rearrange("p t (c n) -> p c t n", n=4),
+            )
+            nc.scalar.copy(
+                out=w_grouped[lag][:, split:LATENT, :].rearrange("p (c n) t -> p c t n", n=4),
+                in_=w_raw[lag][:, :, split:LATENT].rearrange("p t (c n) -> p c t n", n=4),
+            )
+
+        def quantise_wy(lag):
             nc.vector.quantize_mx(
                 out=w_codes[:, lag, :].bitcast(E4M3_X4),
                 scales=w_scales[:, lag, :],
                 in_=w_grouped[lag][:].rearrange("p j t -> p (j t)"),
             )
+
+        def products(lag):
             for i in range(OUT_TILES):
                 slot = i + LAGS - lag
                 columns = slice((slot - 1) * P, slot * P)
@@ -152,11 +131,58 @@ def tile_npchangetransitionprior_pa_s_kernel(tc, x, emb, Wg, bg, grad_out, out):
                     stop=(lag == LAGS - 1),
                 )
 
-        for i in range(3, OUT_TILES):
+        def own_latent_term(i):
+            nc.vector.tensor_tensor(out=own[i][:], in0=g_slots[:, i, :], in1=wx_all[:], op=MULT)
+
+        def finish(i):
+            if i == SIDE_TILE:
+                nc.scalar.copy(out=side_sum[:], in_=acc[i][:])
+                nc.gpsimd.tensor_tensor(out=result[i][:], in0=side_sum[:], in1=own[i][:], op=ADD)
+                nc.scalar.dma_start(out=out_rows[:, i, :], in_=result[i][:])
+            else:
+                nc.vector.tensor_tensor(out=result[i][:], in0=acc[i][:], in1=own[i][:], op=ADD)
+                nc.sync.dma_start(out=out_rows[:, i, :], in_=result[i][:])
+
+        with nc.allow_non_contiguous_dma(reason="wx is one column of Wg: 512 single elements"):
+            nc.scalar.dma_start(
+                out=wx_sb[:],
+                in_=Wg[:, WX_COLUMN : WX_COLUMN + 1].rearrange("(c q) o -> q (c o)", q=P),
+            )
+        nc.vector.memset(g_slots[:, 0:LAGS, :].bitcast(F32), 0.0)
+        nc.vector.memset(g_slots[:, OUT_TILES:SLOTS, :].bitcast(F32), 0.0)
+        load_slots(LAGS, OUT_TILES)
+        load_slots(0, LAGS)
+        load_slots(OUT_TILES, SLOTS)
+        for lag in range(LAGS):
+            load_wy(lag)
+
+        make_identity(nc, ident_bf16[:])
+        make_identity(nc, ident_f32[:])
+        for c in range(PACK):
+            nc.tensor.matmul(
+                out=wx_all[:, c * P : (c + 1) * P],
+                lhsT=wx_sb[:, c : c + 1].to_broadcast([P, P]),
+                rhs=ident_bf16[:],
+                start=True,
+                stop=True,
+            )
+
+        for i in range(LAGS, OUT_TILES):
+            own_latent_term(i)
+        flip_slots(0)
+        regroup_wy(0)
+        flip_slots(1)
+        quantise_slots(0)
+        quantise_wy(0)
+        flip_slots(2)
+        quantise_slots(1)
+        regroup_wy(1)
+        quantise_slots(2)
+        products(0)
+        quantise_wy(1)
+        products(1)
+        for i in range(LAGS):
             own_latent_term(i)
 
-        out_rows = out.rearrange("b (h i) j -> (b h) i j", h=HALVES)
         for i in range(OUT_TILES):
-            result = keep.tile([P, LATENT], F32, name="result%d" % i)
-            nc.vector.tensor_tensor(out=result[:], in0=acc[i][:], in1=own[i][:], op=ADD)
-            nc.sync.dma_start(out=out_rows[:, i, :], in_=result[:])
+            finish(i)

@@ -25,12 +25,14 @@ HALVES = P // BATCH
 OUT_TILES = STEPS_OUT // HALVES
 SLOTS = OUT_TILES + LAGS
 MX_SLOTS = SLOTS - 1
+MX_SLOT_ORDER = list(range(LAGS, SLOTS)) + list(range(1, LAGS))
 
 FLOPS = 2 * BATCH * STEPS_IN * LATENT * LAGS * LATENT
 BYTES = 2 * LATENT * (LAGS * LATENT + 1) + 2 * BATCH * STEPS_IN * LATENT + 4 * BATCH * STEPS_OUT * LATENT
 
 SCALAR_COLUMNS = 160
 SIDE_TILE = 0
+FIRST_ROUND = 3
 
 
 def tile_npchangetransitionprior_pa_s_kernel(tc, x, emb, Wg, bg, grad_out, out):
@@ -47,6 +49,7 @@ def tile_npchangetransitionprior_pa_s_kernel(tc, x, emb, Wg, bg, grad_out, out):
         ident_bf16 = keep.tile([P, P], BF16)
         ident_f32 = keep.tile([P, P], F32)
         wx_all = psum.tile([P, LATENT], F32)
+        wx_copy = keep.tile([P, LATENT], F32)
         g_grouped = keep.tile([P, MX_SLOTS * P, PACK], BF16, align_bytes=64)
         g_codes = keep.tile([P, MX_SLOTS * P], U32, align_bytes=64)
         g_scales = keep.tile([P, MX_SLOTS * P], U8, align_bytes=64)
@@ -56,7 +59,7 @@ def tile_npchangetransitionprior_pa_s_kernel(tc, x, emb, Wg, bg, grad_out, out):
         w_codes = keep.tile([P, LAGS, LATENT], U32, align_bytes=64)
         w_scales = keep.tile([P, LAGS, LATENT], U8, align_bytes=64)
         acc = [psum.tile([P, LATENT], F32, name="acc%d" % i) for i in range(OUT_TILES)]
-        own = [keep.tile([P, LATENT], F32, name="own%d" % i) for i in range(OUT_TILES)]
+        own = keep.tile([P, OUT_TILES, LATENT], F32)
         result = [keep.tile([P, LATENT], F32, name="result%d" % i) for i in range(OUT_TILES)]
         side_sum = keep.tile([P, LATENT], F32)
 
@@ -85,7 +88,7 @@ def tile_npchangetransitionprior_pa_s_kernel(tc, x, emb, Wg, bg, grad_out, out):
             flipped = psum_flip.tile([P, 2, 2, P], F32)
             for n in range(2):
                 for u in range(2):
-                    nc.tensor.transpose(flipped[:, n, u, :], g_words[:, 1 + 2 * pair + n, u, :], ident_f32[:])
+                    nc.tensor.transpose(flipped[:, n, u, :], g_words[:, MX_SLOT_ORDER[2 * pair + n], u, :], ident_f32[:])
             nc.scalar.copy(
                 out=g_grouped_words[:, 2 * pair : 2 * pair + 2, :, :],
                 in_=flipped[:].rearrange("q v u r -> q v r u"),
@@ -117,10 +120,10 @@ def tile_npchangetransitionprior_pa_s_kernel(tc, x, emb, Wg, bg, grad_out, out):
                 in_=w_grouped[lag][:].rearrange("p j t -> p (j t)"),
             )
 
-        def products(lag):
-            for i in range(OUT_TILES):
-                slot = i + LAGS - lag
-                columns = slice((slot - 1) * P, slot * P)
+        def products(lag, tiles):
+            for i in tiles:
+                place = MX_SLOT_ORDER.index(i + LAGS - lag)
+                columns = slice(place * P, (place + 1) * P)
                 nc.tensor.matmul_mx(
                     out=acc[i][:],
                     lhsT=g_codes[:, columns].bitcast(E5M2_X4),
@@ -131,16 +134,21 @@ def tile_npchangetransitionprior_pa_s_kernel(tc, x, emb, Wg, bg, grad_out, out):
                     stop=(lag == LAGS - 1),
                 )
 
-        def own_latent_term(i):
-            nc.vector.tensor_tensor(out=own[i][:], in0=g_slots[:, i, :], in1=wx_all[:], op=MULT)
+        def own_latent_terms(first, end):
+            nc.vector.tensor_tensor(
+                out=own[:, first:end, :],
+                in0=g_slots[:, first:end, :],
+                in1=wx_all[:].unsqueeze(1).to_broadcast([P, end - first, LATENT]),
+                op=MULT,
+            )
 
         def finish(i):
             if i == SIDE_TILE:
                 nc.scalar.copy(out=side_sum[:], in_=acc[i][:])
-                nc.gpsimd.tensor_tensor(out=result[i][:], in0=side_sum[:], in1=own[i][:], op=ADD)
+                nc.gpsimd.tensor_tensor(out=result[i][:], in0=side_sum[:], in1=own[:, i, :], op=ADD)
                 nc.scalar.dma_start(out=out_rows[:, i, :], in_=result[i][:])
             else:
-                nc.vector.tensor_tensor(out=result[i][:], in0=acc[i][:], in1=own[i][:], op=ADD)
+                nc.vector.tensor_tensor(out=result[i][:], in0=acc[i][:], in1=own[:, i, :], op=ADD)
                 nc.sync.dma_start(out=out_rows[:, i, :], in_=result[i][:])
 
         with nc.allow_non_contiguous_dma(reason="wx is one column of Wg: 512 single elements"):
@@ -167,22 +175,26 @@ def tile_npchangetransitionprior_pa_s_kernel(tc, x, emb, Wg, bg, grad_out, out):
                 stop=True,
             )
 
-        for i in range(LAGS, OUT_TILES):
-            own_latent_term(i)
+        nc.scalar.copy(out=wx_copy[:], in_=wx_all[:])
+        nc.gpsimd.tensor_tensor(
+            out=own[:, SIDE_TILE, :], in0=g_slots[:, SIDE_TILE, :], in1=wx_copy[:], op=MULT
+        )
+        own_latent_terms(LAGS, OUT_TILES)
         flip_slots(0)
-        regroup_wy(0)
         flip_slots(1)
         quantise_slots(0)
-        quantise_wy(0)
+        regroup_wy(0)
         flip_slots(2)
         quantise_slots(1)
+        quantise_wy(0)
+        products(0, range(FIRST_ROUND))
         regroup_wy(1)
         quantise_slots(2)
-        products(0)
         quantise_wy(1)
-        products(1)
-        for i in range(LAGS):
-            own_latent_term(i)
+        products(1, range(FIRST_ROUND))
+        for lag in range(LAGS):
+            products(lag, range(FIRST_ROUND, OUT_TILES))
+        own_latent_terms(SIDE_TILE + 1, LAGS)
 
         for i in range(OUT_TILES):
             finish(i)

@@ -31,8 +31,9 @@ FLOPS = 2 * BATCH * STEPS_IN * LATENT * LAGS * LATENT
 BYTES = 2 * LATENT * (LAGS * LATENT + 1) + 2 * BATCH * STEPS_IN * LATENT + 4 * BATCH * STEPS_OUT * LATENT
 
 SCALAR_COLUMNS = 160
-SIDE_TILE = 0
+SIDE_TILE = 1
 FIRST_ROUND = 3
+LAG_ORDER = (1, 0)
 
 
 def tile_npchangetransitionprior_pa_s_kernel(tc, x, emb, Wg, bg, grad_out, out):
@@ -43,12 +44,11 @@ def tile_npchangetransitionprior_pa_s_kernel(tc, x, emb, Wg, bg, grad_out, out):
         psum_flip = ctx.enter_context(tc.psum_pool(name="psum_flip", bufs=2))
         ctx.enter_context(tc.manual_schedule())
 
-        wx_sb = keep.tile([P, PACK], BF16)
         g_slots = keep.tile([P, SLOTS, LATENT], BF16)
-        w_raw = [keep.tile([P, PACK, LATENT], BF16, name="w_raw%d" % lag) for lag in range(LAGS)]
+        w_raw = [keep.tile([P, PACK, LATENT + 2], BF16, name="w_raw%d" % lag) for lag in range(LAGS)]
         ident_bf16 = keep.tile([P, P], BF16)
         ident_f32 = keep.tile([P, P], F32)
-        wx_all = psum.tile([P, LATENT], F32)
+        wx_all = psum.tile([P, PACK, P], F32)
         wx_copy = keep.tile([P, LATENT], F32)
         g_grouped = keep.tile([P, MX_SLOTS * P, PACK], BF16, align_bytes=64)
         g_codes = keep.tile([P, MX_SLOTS * P], U32, align_bytes=64)
@@ -79,9 +79,10 @@ def tile_npchangetransitionprior_pa_s_kernel(tc, x, emb, Wg, bg, grad_out, out):
 
         def load_wy(lag):
             first_column = WY_COLUMN + lag * LATENT
+            columns = LATENT + (1 if lag == LAGS - 1 else 0)
             nc.sync.dma_start(
-                out=w_raw[lag][:],
-                in_=Wg[:, first_column : first_column + LATENT].rearrange("(p t) j -> p t j", t=PACK),
+                out=w_raw[lag][:, :, 0:columns],
+                in_=Wg[:, first_column : first_column + columns].rearrange("(p t) j -> p t j", t=PACK),
             )
 
         def flip_slots(pair):
@@ -120,25 +121,30 @@ def tile_npchangetransitionprior_pa_s_kernel(tc, x, emb, Wg, bg, grad_out, out):
                 in_=w_grouped[lag][:].rearrange("p j t -> p (j t)"),
             )
 
-        def products(lag, tiles):
-            for i in tiles:
-                place = MX_SLOT_ORDER.index(i + LAGS - lag)
-                columns = slice(place * P, (place + 1) * P)
-                nc.tensor.matmul_mx(
-                    out=acc[i][:],
-                    lhsT=g_codes[:, columns].bitcast(E5M2_X4),
-                    lhsT_scale=g_scales[:, columns],
-                    rhs=w_codes[:, lag, :].bitcast(E4M3_X4),
-                    rhs_scale=w_scales[:, lag, :],
-                    start=(lag == 0),
-                    stop=(lag == LAGS - 1),
-                )
+        opened = set()
+
+        def products_of_slot(slot):
+            place = MX_SLOT_ORDER.index(slot)
+            columns = slice(place * P, (place + 1) * P)
+            for lag in LAG_ORDER:
+                i = slot - LAGS + lag
+                if 0 <= i < OUT_TILES:
+                    nc.tensor.matmul_mx(
+                        out=acc[i][:],
+                        lhsT=g_codes[:, columns].bitcast(E5M2_X4),
+                        lhsT_scale=g_scales[:, columns],
+                        rhs=w_codes[:, lag, :].bitcast(E4M3_X4),
+                        rhs_scale=w_scales[:, lag, :],
+                        start=(i not in opened),
+                        stop=(i in opened),
+                    )
+                    opened.add(i)
 
         def own_latent_terms(first, end):
             nc.vector.tensor_tensor(
-                out=own[:, first:end, :],
-                in0=g_slots[:, first:end, :],
-                in1=wx_all[:].unsqueeze(1).to_broadcast([P, end - first, LATENT]),
+                out=own[:, first:end, :].rearrange("r s (n t) -> r s n t", t=PACK),
+                in0=g_slots[:, first:end, :].rearrange("r s (n t) -> r s n t", t=PACK),
+                in1=wx_all[:].rearrange("r t n -> r n t").unsqueeze(1).to_broadcast([P, end - first, P, PACK]),
                 op=MULT,
             )
 
@@ -151,50 +157,45 @@ def tile_npchangetransitionprior_pa_s_kernel(tc, x, emb, Wg, bg, grad_out, out):
                 nc.vector.tensor_tensor(out=result[i][:], in0=acc[i][:], in1=own[:, i, :], op=ADD)
                 nc.sync.dma_start(out=out_rows[:, i, :], in_=result[i][:])
 
-        with nc.allow_non_contiguous_dma(reason="wx is one column of Wg: 512 single elements"):
-            nc.scalar.dma_start(
-                out=wx_sb[:],
-                in_=Wg[:, WX_COLUMN : WX_COLUMN + 1].rearrange("(c q) o -> q (c o)", q=P),
-            )
         nc.vector.memset(g_slots[:, 0:LAGS, :].bitcast(F32), 0.0)
         nc.vector.memset(g_slots[:, OUT_TILES:SLOTS, :].bitcast(F32), 0.0)
+        load_wy(LAG_ORDER[0])
         load_slots(LAGS, OUT_TILES)
         load_slots(0, LAGS)
         load_slots(OUT_TILES, SLOTS)
-        for lag in range(LAGS):
-            load_wy(lag)
+        load_wy(LAG_ORDER[1])
 
         make_identity(nc, ident_bf16[:])
         make_identity(nc, ident_f32[:])
-        for c in range(PACK):
+        for t in range(PACK):
             nc.tensor.matmul(
-                out=wx_all[:, c * P : (c + 1) * P],
-                lhsT=wx_sb[:, c : c + 1].to_broadcast([P, P]),
+                out=wx_all[:, t, :],
+                lhsT=w_raw[LAGS - 1][:, t, LATENT : LATENT + 1].to_broadcast([P, P]),
                 rhs=ident_bf16[:],
                 start=True,
                 stop=True,
             )
 
-        nc.scalar.copy(out=wx_copy[:], in_=wx_all[:])
+        regroup_wy(LAG_ORDER[0])
+        nc.scalar.copy(out=wx_copy[:].rearrange("r (n t) -> r n t", t=PACK), in_=wx_all[:].rearrange("r t n -> r n t"))
         nc.gpsimd.tensor_tensor(
             out=own[:, SIDE_TILE, :], in0=g_slots[:, SIDE_TILE, :], in1=wx_copy[:], op=MULT
         )
+        quantise_wy(LAG_ORDER[0])
         own_latent_terms(LAGS, OUT_TILES)
         flip_slots(0)
         flip_slots(1)
         quantise_slots(0)
-        regroup_wy(0)
+        regroup_wy(LAG_ORDER[1])
         flip_slots(2)
+        quantise_wy(LAG_ORDER[1])
         quantise_slots(1)
-        quantise_wy(0)
-        products(0, range(FIRST_ROUND))
-        regroup_wy(1)
+        for slot in MX_SLOT_ORDER[0:4]:
+            products_of_slot(slot)
+        own_latent_terms(0, SIDE_TILE)
         quantise_slots(2)
-        quantise_wy(1)
-        products(1, range(FIRST_ROUND))
-        for lag in range(LAGS):
-            products(lag, range(FIRST_ROUND, OUT_TILES))
-        own_latent_terms(SIDE_TILE + 1, LAGS)
+        for slot in reversed(MX_SLOT_ORDER[4:6]):
+            products_of_slot(slot)
 
-        for i in range(OUT_TILES):
+        for i in (1, 2, 3, 0, 4):
             finish(i)

@@ -45,7 +45,7 @@ def tile_npchangetransitionprior_pa_s_kernel(tc, x, emb, Wg, bg, grad_out, out):
         ctx.enter_context(tc.manual_schedule())
 
         g_slots = keep.tile([P, SLOTS, LATENT], BF16)
-        w_raw = [keep.tile([P, PACK, LATENT + 2], BF16, name="w_raw%d" % lag) for lag in range(LAGS)]
+        w_raw = [keep.tile([P, PACK, LATENT + 16], BF16, name="w_raw%d" % lag) for lag in range(LAGS)]
         ident_bf16 = keep.tile([P, P], BF16)
         ident_f32 = keep.tile([P, P], F32)
         wx_all = psum.tile([P, PACK, P], F32)

@@ -31,7 +31,7 @@ FLOPS = 2 * BATCH * STEPS_IN * LATENT * LAGS * LATENT
 BYTES = 2 * LATENT * (LAGS * LATENT + 1) + 2 * BATCH * STEPS_IN * LATENT + 4 * BATCH * STEPS_OUT * LATENT
 
 SCALAR_COLUMNS = 160
-SIDE_TILE = 1
+SIDE_TILE = 0
 FIRST_ROUND = 3
 LAG_ORDER = (1, 0)
 
@@ -103,15 +103,10 @@ def tile_npchangetransitionprior_pa_s_kernel(tc, x, emb, Wg, bg, grad_out, out):
                 in_=g_grouped[:, columns, :].rearrange("q r t -> q (r t)"),
             )
 
-        def regroup_wy(lag):
-            split = LATENT - SCALAR_COLUMNS
-            nc.vector.tensor_copy(
-                out=w_grouped[lag][:, 0:split, :].rearrange("p (c n) t -> p c t n", n=4),
-                in_=w_raw[lag][:, :, 0:split].rearrange("p t (c n) -> p c t n", n=4),
-            )
-            nc.scalar.copy(
-                out=w_grouped[lag][:, split:LATENT, :].rearrange("p (c n) t -> p c t n", n=4),
-                in_=w_raw[lag][:, :, split:LATENT].rearrange("p t (c n) -> p c t n", n=4),
+        def regroup_wy(lag, engine_copy, first, end):
+            engine_copy(
+                out=w_grouped[lag][:, first:end, :].rearrange("p (c n) t -> p c t n", n=4),
+                in_=w_raw[lag][:, :, first:end].rearrange("p t (c n) -> p c t n", n=4),
             )
 
         def quantise_wy(lag):
@@ -121,24 +116,19 @@ def tile_npchangetransitionprior_pa_s_kernel(tc, x, emb, Wg, bg, grad_out, out):
                 in_=w_grouped[lag][:].rearrange("p j t -> p (j t)"),
             )
 
-        opened = set()
-
-        def products_of_slot(slot):
-            place = MX_SLOT_ORDER.index(slot)
-            columns = slice(place * P, (place + 1) * P)
-            for lag in LAG_ORDER:
-                i = slot - LAGS + lag
-                if 0 <= i < OUT_TILES:
-                    nc.tensor.matmul_mx(
-                        out=acc[i][:],
-                        lhsT=g_codes[:, columns].bitcast(E5M2_X4),
-                        lhsT_scale=g_scales[:, columns],
-                        rhs=w_codes[:, lag, :].bitcast(E4M3_X4),
-                        rhs_scale=w_scales[:, lag, :],
-                        start=(i not in opened),
-                        stop=(i in opened),
-                    )
-                    opened.add(i)
+        def products(lag, tiles):
+            for i in tiles:
+                place = MX_SLOT_ORDER.index(i + LAGS - lag)
+                columns = slice(place * P, (place + 1) * P)
+                nc.tensor.matmul_mx(
+                    out=acc[i][:],
+                    lhsT=g_codes[:, columns].bitcast(E5M2_X4),
+                    lhsT_scale=g_scales[:, columns],
+                    rhs=w_codes[:, lag, :].bitcast(E4M3_X4),
+                    rhs_scale=w_scales[:, lag, :],
+                    start=(lag == LAG_ORDER[0]),
+                    stop=(lag == LAG_ORDER[-1]),
+                )
 
         def own_latent_terms(first, end):
             nc.vector.tensor_tensor(
@@ -176,26 +166,28 @@ def tile_npchangetransitionprior_pa_s_kernel(tc, x, emb, Wg, bg, grad_out, out):
                 stop=True,
             )
 
-        regroup_wy(LAG_ORDER[0])
+        split = LATENT - SCALAR_COLUMNS
+        regroup_wy(LAG_ORDER[0], nc.vector.tensor_copy, 0, split)
+        regroup_wy(LAG_ORDER[0], nc.scalar.copy, split, LATENT)
         nc.scalar.copy(out=wx_copy[:].rearrange("r (n t) -> r n t", t=PACK), in_=wx_all[:].rearrange("r t n -> r n t"))
         nc.gpsimd.tensor_tensor(
             out=own[:, SIDE_TILE, :], in0=g_slots[:, SIDE_TILE, :], in1=wx_copy[:], op=MULT
         )
+        own_latent_terms(2, 4)
+        own_latent_terms(1, 2)
         quantise_wy(LAG_ORDER[0])
-        own_latent_terms(LAGS, OUT_TILES)
         flip_slots(0)
-        flip_slots(1)
         quantise_slots(0)
-        regroup_wy(LAG_ORDER[1])
+        regroup_wy(LAG_ORDER[1], nc.vector.tensor_copy, 0, split)
+        regroup_wy(LAG_ORDER[1], nc.scalar.copy, split, LATENT)
+        flip_slots(1)
         flip_slots(2)
-        quantise_wy(LAG_ORDER[1])
         quantise_slots(1)
-        for slot in MX_SLOT_ORDER[0:4]:
-            products_of_slot(slot)
-        own_latent_terms(0, SIDE_TILE)
+        quantise_wy(LAG_ORDER[1])
         quantise_slots(2)
-        for slot in reversed(MX_SLOT_ORDER[4:6]):
-            products_of_slot(slot)
+        products(LAG_ORDER[0], (1, 2, 3, 4, 0))
+        products(LAG_ORDER[1], range(OUT_TILES))
+        own_latent_terms(4, 5)
 
-        for i in (1, 2, 3, 0, 4):
+        for i in range(OUT_TILES):
             finish(i)

@@ -31,7 +31,7 @@ FLOPS = 2 * BATCH * STEPS_IN * LATENT * LAGS * LATENT
 BYTES = 2 * LATENT * (LAGS * LATENT + 1) + 2 * BATCH * STEPS_IN * LATENT + 4 * BATCH * STEPS_OUT * LATENT
 
 SCALAR_COLUMNS = 160
-SIDE_TILE = 0
+SIDE_TILE = 1
 FIRST_ROUND = 3
 LAG_ORDER = (1, 0)
 
@@ -116,6 +116,8 @@ def tile_npchangetransitionprior_pa_s_kernel(tc, x, emb, Wg, bg, grad_out, out):
                 in_=w_grouped[lag][:].rearrange("p j t -> p (j t)"),
             )
 
+        opened = set()
+
         def products(lag, tiles):
             for i in tiles:
                 place = MX_SLOT_ORDER.index(i + LAGS - lag)
@@ -126,9 +128,10 @@ def tile_npchangetransitionprior_pa_s_kernel(tc, x, emb, Wg, bg, grad_out, out):
                     lhsT_scale=g_scales[:, columns],
                     rhs=w_codes[:, lag, :].bitcast(E4M3_X4),
                     rhs_scale=w_scales[:, lag, :],
-                    start=(lag == LAG_ORDER[0]),
-                    stop=(lag == LAG_ORDER[-1]),
+                    start=(i not in opened),
+                    stop=(i in opened),
                 )
+                opened.add(i)
 
         def own_latent_terms(first, end):
             nc.vector.tensor_tensor(
@@ -174,7 +177,6 @@ def tile_npchangetransitionprior_pa_s_kernel(tc, x, emb, Wg, bg, grad_out, out):
             out=own[:, SIDE_TILE, :], in0=g_slots[:, SIDE_TILE, :], in1=wx_copy[:], op=MULT
         )
         own_latent_terms(2, 4)
-        own_latent_terms(1, 2)
         quantise_wy(LAG_ORDER[0])
         flip_slots(0)
         quantise_slots(0)
@@ -184,10 +186,13 @@ def tile_npchangetransitionprior_pa_s_kernel(tc, x, emb, Wg, bg, grad_out, out):
         flip_slots(2)
         quantise_slots(1)
         quantise_wy(LAG_ORDER[1])
+        products(1, (1, 2, 3, 4))
+        products(0, (1, 2, 3, 0))
         quantise_slots(2)
-        products(LAG_ORDER[0], (1, 2, 3, 4, 0))
-        products(LAG_ORDER[1], range(OUT_TILES))
+        products(1, (0,))
+        products(0, (4,))
         own_latent_terms(4, 5)
+        own_latent_terms(0, 1)
 
-        for i in range(OUT_TILES):
+        for i in (1, 2, 3, 0, 4):
             finish(i)

@@ -62,6 +62,7 @@ def tile_npchangetransitionprior_pa_s_kernel(tc, x, emb, Wg, bg, grad_out, out):
         own = keep.tile([P, OUT_TILES, LATENT], F32)
         result = [keep.tile([P, LATENT], F32, name="result%d" % i) for i in range(OUT_TILES)]
         side_sum = keep.tile([P, LATENT], F32)
+        gate_word = keep.tile([P, 1], U32)
 
         g_words = g_slots[:].bitcast(F32).rearrange("r v (q u) -> r v u q", u=2)
         g_grouped_words = g_grouped[:].bitcast(F32).rearrange("q (v r) u -> q v r u", r=P)
@@ -192,7 +193,8 @@ def tile_npchangetransitionprior_pa_s_kernel(tc, x, emb, Wg, bg, grad_out, out):
         products(1, (0,))
         products(0, (4,))
         own_latent_terms(4, 5)
-        own_latent_terms(0, 1)
+        nc.gpsimd.tensor_copy(out=gate_word[:], in_=g_codes[:, MX_SLOTS * P - 1 : MX_SLOTS * P])
+        nc.gpsimd.tensor_tensor(out=own[:, 0, :], in0=g_slots[:, 0, :], in1=wx_copy[:], op=MULT)
 
         for i in (1, 2, 3, 0, 4):
             finish(i)

@@ -63,8 +63,10 @@ def tile_npchangetransitionprior_pa_s_kernel(tc, x, emb, Wg, bg, grad_out, out):
         result = [keep.tile([P, LATENT], F32, name="result%d" % i) for i in range(OUT_TILES)]
         side_sum = keep.tile([P, LATENT], F32)
         gate_word = keep.tile([P, 1], U32)
+        table_in = keep.tile([P, 1], F32)
+        table_out = keep.tile([P, 1], F32)
 
-        g_words = g_slots[:].bitcast(F32).rearrange("r v (q u) -> r v u q", u=2)
+        g_words = g_slots[:].bitcast(F32).rearrange("r v (u q) -> r v u q", u=2)
         g_grouped_words = g_grouped[:].bitcast(F32).rearrange("q (v r) u -> q v r u", r=P)
         out_rows = out.rearrange("b (h i) j -> (b h) i j", h=HALVES)
 
@@ -81,10 +83,13 @@ def tile_npchangetransitionprior_pa_s_kernel(tc, x, emb, Wg, bg, grad_out, out):
         def load_wy(lag):
             first_column = WY_COLUMN + lag * LATENT
             columns = LATENT + (1 if lag == LAGS - 1 else 0)
-            nc.sync.dma_start(
-                out=w_raw[lag][:, :, 0:columns],
-                in_=Wg[:, first_column : first_column + columns].rearrange("(p t) j -> p t j", t=PACK),
-            )
+            for u in range(2):
+                nc.sync.dma_start(
+                    out=w_raw[lag][:, 2 * u : 2 * u + 2, 0:columns],
+                    in_=Wg[256 * u : 256 * (u + 1), first_column : first_column + columns].rearrange(
+                        "(p e) j -> p e j", e=2
+                    ),
+                )
 
         def flip_slots(pair):
             flipped = psum_flip.tile([P, 2, 2, P], F32)
@@ -135,12 +140,13 @@ def tile_npchangetransitionprior_pa_s_kernel(tc, x, emb, Wg, bg, grad_out, out):
                 opened.add(i)
 
         def own_latent_terms(first, end):
-            nc.vector.tensor_tensor(
-                out=own[:, first:end, :].rearrange("r s (n t) -> r s n t", t=PACK),
-                in0=g_slots[:, first:end, :].rearrange("r s (n t) -> r s n t", t=PACK),
-                in1=wx_all[:].rearrange("r t n -> r n t").unsqueeze(1).to_broadcast([P, end - first, P, PACK]),
-                op=MULT,
-            )
+            for s in range(first, end):
+                nc.vector.tensor_tensor(
+                    out=own[:, s, :].rearrange("r (u n e) -> r u n e", u=2, e=2),
+                    in0=g_slots[:, s, :].rearrange("r (u n e) -> r u n e", u=2, e=2),
+                    in1=wx_all[:].rearrange("r (u e) n -> r u n e", u=2),
+                    op=MULT,
+                )
 
         def finish(i):
             if i == SIDE_TILE:
@@ -151,6 +157,8 @@ def tile_npchangetransitionprior_pa_s_kernel(tc, x, emb, Wg, bg, grad_out, out):
                 nc.vector.tensor_tensor(out=result[i][:], in0=acc[i][:], in1=own[:, i, :], op=ADD)
                 nc.sync.dma_start(out=out_rows[:, i, :], in_=result[i][:])
 
+        nc.vector.memset(table_in[:], 0.0)
+        nc.scalar.copy(out=table_out[:], in_=table_in[:])
         nc.vector.memset(g_slots[:, 0:LAGS, :].bitcast(F32), 0.0)
         nc.vector.memset(g_slots[:, OUT_TILES:SLOTS, :].bitcast(F32), 0.0)
         load_wy(LAG_ORDER[0])
@@ -173,7 +181,9 @@ def tile_npchangetransitionprior_pa_s_kernel(tc, x, emb, Wg, bg, grad_out, out):
         split = LATENT - SCALAR_COLUMNS
         regroup_wy(LAG_ORDER[0], nc.vector.tensor_copy, 0, split)
         regroup_wy(LAG_ORDER[0], nc.scalar.copy, split, LATENT)
-        nc.scalar.copy(out=wx_copy[:].rearrange("r (n t) -> r n t", t=PACK), in_=wx_all[:].rearrange("r t n -> r n t"))
+        nc.scalar.copy(
+            out=wx_copy[:].rearrange("r (u n e) -> r u n e", u=2, e=2), in_=wx_all[:].rearrange("r (u e) n -> r u n e", u=2)
+        )
         nc.gpsimd.tensor_tensor(
             out=own[:, SIDE_TILE, :], in0=g_slots[:, SIDE_TILE, :], in1=wx_copy[:], op=MULT
         )

from contextlib import ExitStack

import concourse.mybir as mybir
from concourse.masks import make_identity

F32 = mybir.dt.float32
BF16 = mybir.dt.bfloat16
U32 = mybir.dt.uint32
U8 = mybir.dt.uint8
E4M3_X4 = mybir.dt.float8_e4m3fn_x4
E5M2_X4 = mybir.dt.float8_e5m2_x4
MULT = mybir.AluOpType.mult
ADD = mybir.AluOpType.add

P = 128
PACK = 4
BATCH = 64
STEPS_IN = 8
STEPS_OUT = 10
LATENT = 512
LAGS = 2
WY_COLUMN = 128
WX_COLUMN = WY_COLUMN + LAGS * LATENT
HALVES = P // BATCH
OUT_TILES = STEPS_OUT // HALVES
SLOTS = OUT_TILES + LAGS
MX_SLOTS = SLOTS - 1
MX_SLOT_ORDER = list(range(LAGS, SLOTS)) + list(range(1, LAGS))

FLOPS = 2 * BATCH * STEPS_IN * LATENT * LAGS * LATENT
BYTES = 2 * LATENT * (LAGS * LATENT + 1) + 2 * BATCH * STEPS_IN * LATENT + 4 * BATCH * STEPS_OUT * LATENT

SCALAR_COLUMNS = 160
SIDE_TILE = 1
FIRST_ROUND = 3
LAG_ORDER = (1, 0)


def tile_npchangetransitionprior_pa_s_kernel(tc, x, emb, Wg, bg, grad_out, out):
    nc = tc.nc
    with ExitStack() as ctx:
        keep = ctx.enter_context(tc.tile_pool(name="keep", bufs=1))
        psum = ctx.enter_context(tc.psum_pool(name="psum", bufs=1))
        psum_flip = ctx.enter_context(tc.psum_pool(name="psum_flip", bufs=2))
        ctx.enter_context(tc.manual_schedule())

        g_slots = keep.tile([P, SLOTS, LATENT], BF16)
        w_raw = [keep.tile([P, PACK, LATENT + 16], BF16, name="w_raw%d" % lag) for lag in range(LAGS)]
        ident_bf16 = keep.tile([P, P], BF16)
        ident_f32 = keep.tile([P, P], F32)
        wx_all = psum.tile([P, PACK, P], F32)
        wx_copy = keep.tile([P, LATENT], F32)
        g_grouped = keep.tile([P, MX_SLOTS * P, PACK], BF16, align_bytes=64)
        g_codes = keep.tile([P, MX_SLOTS * P], U32, align_bytes=64)
        g_scales = keep.tile([P, MX_SLOTS * P], U8, align_bytes=64)
        w_grouped = [
            keep.tile([P, LATENT, PACK], BF16, name="w_grouped%d" % lag, align_bytes=64) for lag in range(LAGS)
        ]
        w_codes = keep.tile([P, LAGS, LATENT], U32, align_bytes=64)
        w_scales = keep.tile([P, LAGS, LATENT], U8, align_bytes=64)
        acc = [psum.tile([P, LATENT], F32, name="acc%d" % i) for i in range(OUT_TILES)]
        own = keep.tile([P, OUT_TILES, LATENT], F32)
        result = [keep.tile([P, LATENT], F32, name="result%d" % i) for i in range(OUT_TILES)]
        side_sum = keep.tile([P, LATENT], F32)
        gate_word = keep.tile([P, 1], U32)
        table_in = keep.tile([P, 1], F32)
        table_out = keep.tile([P, 1], F32)

        g_words = g_slots[:].bitcast(F32).rearrange("r v (u q) -> r v u q", u=2)
        g_grouped_words = g_grouped[:].bitcast(F32).rearrange("q (v r) u -> q v r u", r=P)
        out_rows = out.rearrange("b (h i) j -> (b h) i j", h=HALVES)

        def load_slots(first_slot, end_slot):
            for h in range(HALVES):
                first_step = h * OUT_TILES - LAGS + first_slot
                end_step = h * OUT_TILES - LAGS + end_slot
                if 0 <= first_step and end_step <= STEPS_IN:
                    nc.sync.dma_start(
                        out=g_slots[h:P:HALVES, first_slot:end_slot, :],
                        in_=grad_out[:, first_step:end_step, :],
                    )

        def load_wy(lag):
            first_column = WY_COLUMN + lag * LATENT
            columns = LATENT + (1 if lag == LAGS - 1 else 0)
            for u in range(2):
                nc.sync.dma_start(
                    out=w_raw[lag][:, 2 * u : 2 * u + 2, 0:columns],
                    in_=Wg[256 * u : 256 * (u + 1), first_column : first_column + columns].rearrange(
                        "(p e) j -> p e j", e=2
                    ),
                )

        def flip_slots(pair):
            flipped = psum_flip.tile([P, 2, 2, P], F32)
            for n in range(2):
                for u in range(2):
                    nc.tensor.transpose(flipped[:, n, u, :], g_words[:, MX_SLOT_ORDER[2 * pair + n], u, :], ident_f32[:])
            nc.scalar.copy(
                out=g_grouped_words[:, 2 * pair : 2 * pair + 2, :, :],
                in_=flipped[:].rearrange("q v u r -> q v r u"),
            )

        def quantise_slots(pair):
            columns = slice(2 * pair * P, (2 * pair + 2) * P)
            nc.vector.quantize_mx(
                out=g_codes[:, columns].bitcast(E5M2_X4),
                scales=g_scales[:, columns],
                in_=g_grouped[:, columns, :].rearrange("q r t -> q (r t)"),
            )

        def regroup_wy(lag, engine_copy, first, end):
            engine_copy(
                out=w_grouped[lag][:, first:end, :].rearrange("p (c n) t -> p c t n", n=4),
                in_=w_raw[lag][:, :, first:end].rearrange("p t (c n) -> p c t n", n=4),
            )

        def quantise_wy(lag):
            nc.vector.quantize_mx(
                out=w_codes[:, lag, :].bitcast(E4M3_X4),
                scales=w_scales[:, lag, :],
                in_=w_grouped[lag][:].rearrange("p j t -> p (j t)"),
            )

        opened = set()

        def products(lag, tiles):
            for i in tiles:
                place = MX_SLOT_ORDER.index(i + LAGS - lag)
                columns = slice(place * P, (place + 1) * P)
                nc.tensor.matmul_mx(
                    out=acc[i][:],
                    lhsT=g_codes[:, columns].bitcast(E5M2_X4),
                    lhsT_scale=g_scales[:, columns],
                    rhs=w_codes[:, lag, :].bitcast(E4M3_X4),
                    rhs_scale=w_scales[:, lag, :],
                    start=(i not in opened),
                    stop=(i in opened),
                )
                opened.add(i)

        def own_latent_terms(first, end):
            for s in range(first, end):
                nc.vector.tensor_tensor(
                    out=own[:, s, :].rearrange("r (u n e) -> r u n e", u=2, e=2),
                    in0=g_slots[:, s, :].rearrange("r (u n e) -> r u n e", u=2, e=2),
                    in1=wx_all[:].rearrange("r (u e) n -> r u n e", u=2),
                    op=MULT,
                )

        def finish(i):
            if i == SIDE_TILE:
                nc.scalar.copy(out=side_sum[:], in_=acc[i][:])
                nc.gpsimd.tensor_tensor(out=result[i][:], in0=side_sum[:], in1=own[:, i, :], op=ADD)
                nc.scalar.dma_start(out=out_rows[:, i, :], in_=result[i][:])
            else:
                nc.vector.tensor_tensor(out=result[i][:], in0=acc[i][:], in1=own[:, i, :], op=ADD)
                nc.sync.dma_start(out=out_rows[:, i, :], in_=result[i][:])

        nc.vector.memset(table_in[:], 0.0)
        nc.scalar.copy(out=table_out[:], in_=table_in[:])
        nc.vector.memset(g_slots[:, 0:LAGS, :].bitcast(F32), 0.0)
        nc.vector.memset(g_slots[:, OUT_TILES:SLOTS, :].bitcast(F32), 0.0)
        load_wy(LAG_ORDER[0])
        load_slots(LAGS, OUT_TILES)
        load_slots(0, LAGS)
        load_slots(OUT_TILES, SLOTS)
        load_wy(LAG_ORDER[1])

        make_identity(nc, ident_bf16[:])
        make_identity(nc, ident_f32[:])
        for t in range(PACK):
            nc.tensor.matmul(
                out=wx_all[:, t, :],
                lhsT=w_raw[LAGS - 1][:, t, LATENT : LATENT + 1].to_broadcast([P, P]),
                rhs=ident_bf16[:],
                start=True,
                stop=True,
            )

        split = LATENT - SCALAR_COLUMNS
        regroup_wy(LAG_ORDER[0], nc.vector.tensor_copy, 0, split)
        regroup_wy(LAG_ORDER[0], nc.scalar.copy, split, LATENT)
        nc.scalar.copy(
            out=wx_copy[:].rearrange("r (u n e) -> r u n e", u=2, e=2), in_=wx_all[:].rearrange("r (u e) n -> r u n e", u=2)
        )
        nc.gpsimd.tensor_tensor(
            out=own[:, SIDE_TILE, :], in0=g_slots[:, SIDE_TILE, :], in1=wx_copy[:], op=MULT
        )
        own_latent_terms(2, 4)
        quantise_wy(LAG_ORDER[0])
        flip_slots(0)
        quantise_slots(0)
        regroup_wy(LAG_ORDER[1], nc.vector.tensor_copy, 0, split)
        regroup_wy(LAG_ORDER[1], nc.scalar.copy, split, LATENT)
        flip_slots(1)
        flip_slots(2)
        quantise_slots(1)
        quantise_wy(LAG_ORDER[1])
        products(1, (1, 2, 3, 4))
        products(0, (1, 2, 3, 0))
        quantise_slots(2)
        products(1, (0,))
        products(0, (4,))
        own_latent_terms(4, 5)
        nc.gpsimd.tensor_copy(out=gate_word[:], in_=g_codes[:, MX_SLOTS * P - 1 : MX_SLOTS * P])
        nc.gpsimd.tensor_tensor(out=own[:, 0, :], in0=g_slots[:, 0, :], in1=wx_copy[:], op=MULT)

        for i in (1, 2, 3, 0, 4):
            finish(i)
